import numpy as np
import ml_dtypes


def mxq(x, axis, fmt="e4m3"):
    dtype, down = {"e4m3": (ml_dtypes.float8_e4m3fn, 7), "e5m2": (ml_dtypes.float8_e5m2, 14)}[fmt]
    v = np.moveaxis(np.asarray(x, np.float32).astype(ml_dtypes.bfloat16).astype(np.float64), axis, -1)
    blocks = v.reshape(v.shape[:-1] + (-1, 32))
    amax = np.abs(blocks).max(-1, keepdims=True)
    byte = np.maximum(np.where(amax > 0, np.frexp(amax)[1] - 1 + 127, 0) - down, 1)
    scale = np.exp2(byte - 127.0)
    codes = (blocks / scale).astype(np.float32).astype(dtype).astype(np.float64)
    return np.moveaxis((codes * scale).reshape(v.shape), -1, axis)


WIDE = False


def mx_kscale(k):
    if not WIDE:
        return np.ones(k)
    levels = np.array([10, -10, 5, -5, 0])
    a = np.random.permutation(np.resize(levels, k // 512 * 4)).reshape(k // 512, 4)
    idx = np.arange(k)
    return np.exp2(a[idx // 512, idx % 128 // 32])


BF16 = ml_dtypes.bfloat16


def bf(x):
    return np.asarray(x, np.float32).astype(BF16)


def f64(x):
    return np.asarray(x).astype(np.float64)


E2M1 = np.array([0.0, 0.5, 1.0, 1.5, 2.0, 3.0, 4.0, 6.0, -0.0, -0.5, -1.0, -1.5, -2.0, -3.0, -4.0, -6.0])


def pack_weight(w, fmt):
    k, n = w.shape
    w = f64(bf(w)).reshape(k // 32, 32, n)
    amax = np.abs(w).max(1)
    if fmt == "e4m3":
        byte = np.frexp(amax)[1] - 1 + 127 - 7
    else:
        mant, ex = np.frexp(amax / 6.0)
        byte = np.where(mant > 0.5, ex, ex - 1) + 127
    byte = np.clip(np.where(amax > 0, byte, 1), 1, 254)
    scaled = (w * np.exp2(127.0 - byte)[:, None, :]).reshape(k, n).astype(np.float32)
    by_word = np.ascontiguousarray(scaled.reshape(k // 512, 128, 4, n).transpose(0, 1, 3, 2))
    if fmt == "e4m3":
        words = by_word.astype(ml_dtypes.float8_e4m3fn).view(np.uint8)
    else:
        c = by_word.astype(ml_dtypes.float4_e2m1fn).view(np.uint8) & 0xF
        words = c[..., 0::2] | (c[..., 1::2] << 4)
    return np.ascontiguousarray(words), np.ascontiguousarray(byte.astype(np.uint8).reshape(k // 512, 16, n))


def unpack_weight(words, scales, fmt):
    g, p, n, _ = words.shape
    if fmt == "e4m3":
        vals = np.ascontiguousarray(words).view(ml_dtypes.float8_e4m3fn).astype(np.float64)
    else:
        nib = np.empty((g, p, n, 4), np.uint8)
        nib[..., 0::2] = words & 0xF
        nib[..., 1::2] = words >> 4
        vals = E2M1[nib]
    vals = vals * np.repeat(np.exp2(scales.astype(np.float64) - 127.0), 8, axis=1)[..., None]
    return vals.transpose(0, 1, 3, 2).reshape(g * 512, n)


T, H, NQ, NKV, HD = 512, 2048, 32, 2, 128
RD = HD // 2
QS, KS = NQ * HD, NKV * HD
OUT = QS + 2 * KS


def extract_rope(x):
    r = x[..., :RD]
    r = r.reshape(*r.shape[:-1], RD // 2, 2)
    return np.swapaxes(r, -2, -1).reshape(*x.shape[:-1], RD)


def fill_rope(x, rope):
    r = rope.reshape(*rope.shape[:-1], 2, RD // 2)
    r = np.swapaxes(r, -2, -1).reshape(*rope.shape)
    return np.concatenate([r, x[..., RD:]], axis=-1)


def rotate_half(x):
    half = x.shape[-1] // 2
    return np.concatenate([-x[..., half:], x[..., :half]], axis=-1)


def setup_inputs():
    s = mx_kscale(H)
    ang = np.random.uniform(0.0, 2.0 * np.pi, (T, RD))
    hidden_states = bf(np.random.standard_normal((T, H)) * s)
    words, scales = pack_weight(np.random.standard_normal((H, OUT)) / np.sqrt(H) / s[:, None], 'e4m3')
    b_qkv = bf(np.random.standard_normal(OUT) * 0.3)
    return {'hidden_states': hidden_states,
            'cos': bf(np.cos(ang)), 'sin': bf(np.sin(ang)),
            'W_qkv_words': words, 'W_qkv_scales': scales,
            'b_qkv': b_qkv}


def reference(hidden_states, cos, sin, W_qkv_words, W_qkv_scales, b_qkv):
    qkv = (mxq(f64(hidden_states), 1, 'e4m3') @ unpack_weight(W_qkv_words, W_qkv_scales, 'e4m3')) + f64(b_qkv)
    q = qkv[:, :QS].reshape(T, NQ, HD)
    k = qkv[:, QS:QS + KS].reshape(T, NKV, HD)
    v = qkv[:, QS + KS:].reshape(T, NKV, HD)
    cos_b = f64(cos)[:, None, :]
    sin_b = f64(sin)[:, None, :]
    q_r = extract_rope(q)
    k_r = extract_rope(k)
    q_r = q_r * cos_b + rotate_half(q_r) * sin_b
    k_r = k_r * cos_b + rotate_half(k_r) * sin_b
    q = fill_rope(q, q_r)
    k = fill_rope(k, k_r)
    return q, k, v

@@ -1,0 +1,191 @@
+from contextlib import ExitStack
+
+import concourse.mybir as mybir
+from concourse.masks import make_identity
+
+F32 = mybir.dt.float32
+BF16 = mybir.dt.bfloat16
+I32 = mybir.dt.int32
+U32 = mybir.dt.uint32
+U8 = mybir.dt.uint8
+FP8X4 = mybir.dt.float8_e4m3fn_x4
+ADD = mybir.AluOpType.add
+MULT = mybir.AluOpType.mult
+
+P = 128
+T, H = 512, 2048
+NQ, NKV, HD = 32, 2, 128
+RD = HD // 2
+QS, KS = NQ * HD, NKV * HD
+OUT = QS + 2 * KS
+K_PASS = 4 * P
+PASSES = H // K_PASS
+TOK_TILES = T // P
+N_BLOCK = 512
+BLOCKS = OUT // N_BLOCK
+BLOCK_HEADS = N_BLOCK // HD
+WORDS = K_PASS // 2
+
+FLOPS = 2 * T * H * OUT
+
+assert QS % N_BLOCK == 0 and 2 * KS == N_BLOCK
+
+
+def tile_selfattention_pa_kernel(
+    tc, hidden_states, cos, sin, W_qkv_words, W_qkv_scales, b_qkv, out_0, out_1, out_2
+):
+    nc = tc.nc
+    with ExitStack() as stack:
+        const = stack.enter_context(tc.tile_pool(name="const", bufs=1))
+        x_pool = stack.enter_context(tc.tile_pool(name="x", bufs=TOK_TILES))
+        grouped_pool = stack.enter_context(tc.tile_pool(name="grouped", bufs=2))
+        w_pool = stack.enter_context(tc.tile_pool(name="w", bufs=BLOCKS * PASSES))
+        y_pool = stack.enter_context(tc.tile_pool(name="y", bufs=12))
+        products_pool = stack.enter_context(tc.tile_pool(name="products", bufs=4))
+        banks = stack.enter_context(tc.psum_pool(name="banks", bufs=7))
+        table_bank = stack.enter_context(tc.psum_pool(name="table_bank", bufs=1))
+
+        w_planes = const.tile([P, OUT], U8, align_bytes=64)
+        nc.vector.memset(w_planes[:].bitcast(I32), 0)
+        bias_row = const.tile([P, OUT], BF16)
+        nc.vector.memset(bias_row[:].bitcast(I32), 0)
+
+        x_tiles = []
+        for m in range(TOK_TILES):
+            x_sb = x_pool.tile([P, H], BF16)
+            nc.sync.dma_start(out=x_sb[:], in_=hidden_states[m * P : (m + 1) * P, :])
+            x_tiles.append(x_sb)
+        for quad in range(4):
+            nc.sync.dma_start(
+                out=w_planes[32 * quad : 32 * quad + 16, :].bitcast(I32),
+                in_=W_qkv_scales[:, 4 * quad : 4 * quad + 4, :].bitcast(I32),
+            )
+        w_tiles = {}
+        for c in range(BLOCKS):
+            for g in range(PASSES):
+                w_sb = w_pool.tile([P, N_BLOCK], U32, align_bytes=64)
+                w_bytes = W_qkv_words[g].rearrange("p n t -> p (n t)")
+                nc.sync.dma_start(
+                    out=w_sb[:].bitcast(I32),
+                    in_=w_bytes[:, 4 * c * N_BLOCK : 4 * (c + 1) * N_BLOCK].bitcast(I32),
+                )
+                w_tiles[(c, g)] = w_sb
+
+        nc.scalar.dma_start(out=bias_row[0:1, :], in_=b_qkv.unsqueeze(0))
+        cos_sb = const.tile([P, TOK_TILES, RD], BF16)
+        sin_sb = const.tile([P, TOK_TILES, RD], BF16)
+        nc.scalar.dma_start(out=cos_sb[:], in_=cos.rearrange("(m p) c -> p m c", p=P))
+        nc.scalar.dma_start(out=sin_sb[:], in_=sin.rearrange("(m p) c -> p m c", p=P))
+
+        ident_f32 = const.tile([P, P], F32)
+        make_identity(nc, ident_f32[:])
+        ident_bf16 = const.tile([P, P], BF16)
+        make_identity(nc, ident_bf16[:])
+        ones = const.tile([P, P], BF16)
+        nc.vector.memset(ones[:], 1.0)
+
+        x_codes = const.tile([P, TOK_TILES, PASSES, P], U32, align_bytes=64)
+        x_scales = const.tile([P, TOK_TILES, PASSES, P], U8, align_bytes=64)
+        for m in range(TOK_TILES):
+            x_words = x_tiles[m][:].bitcast(F32)
+            grouped = grouped_pool.tile([P, PASSES, P, 4], BF16, align_bytes=64)
+            grouped_flat = grouped[:].rearrange("p g r t -> p (g r t)")
+            grouped_words = grouped_flat.bitcast(F32).rearrange(
+                "p (g r u) -> p g r u", g=PASSES, u=2
+            )
+            for half in range(2):
+                xt = banks.tile([P, 2, 2, P], F32, tag="bank")
+                for a in range(2):
+                    g = 2 * half + a
+                    for u in range(2):
+                        nc.tensor.transpose(
+                            xt[:, a, u, :],
+                            x_words[:, WORDS * g + u : WORDS * (g + 1) : 2],
+                            ident_f32[:],
+                        )
+                copy_out = nc.scalar.copy if half == 0 else nc.vector.tensor_copy
+                copy_out(
+                    out=grouped_words[:, 2 * half : 2 * half + 2, :, :],
+                    in_=xt[:].rearrange("p a u r -> p a r u"),
+                )
+            nc.vector.quantize_mx(
+                out=x_codes[:, m].rearrange("p g r -> p (g r)").bitcast(FP8X4),
+                scales=x_scales[:, m].rearrange("p g r -> p (g r)"),
+                in_=grouped_flat,
+            )
+
+        table_sb = const.tile([P, TOK_TILES, RD, 2], BF16)
+        table_js = table_sb[:].rearrange("p m (j s) e -> p m j s e", s=2)
+        half_rd = RD // 2
+        nc.vector.tensor_copy(out=table_js[:, :, :, 0, 0], in_=cos_sb[:, :, 0:half_rd])
+        nc.vector.tensor_copy(out=table_js[:, :, :, 0, 1], in_=sin_sb[:, :, half_rd:RD])
+        nc.vector.tensor_scalar_mul(
+            out=table_js[:, :, :, 1, 0], in0=sin_sb[:, :, 0:half_rd], scalar1=-1.0
+        )
+        nc.vector.tensor_copy(out=table_js[:, :, :, 1, 1], in_=cos_sb[:, :, half_rd:RD])
+        table_ps = table_bank.tile([P, TOK_TILES, RD, 2], F32)
+        nc.tensor.matmul(
+            out=table_ps[:].rearrange("p m i e -> p (m i e)"),
+            lhsT=ident_bf16[:],
+            rhs=table_sb[:].rearrange("p m i e -> p (m i e)"),
+            start=True,
+            stop=True,
+        )
+
+        bias_sb = const.tile([P, OUT], F32)
+        for c in range(BLOCKS):
+            cols = slice(c * N_BLOCK, (c + 1) * N_BLOCK)
+            spread = banks.tile([P, N_BLOCK], F32, tag="bank")
+            nc.tensor.matmul(out=spread[:], lhsT=ones[:], rhs=bias_row[:, cols], start=True, stop=True)
+            copy_out = nc.scalar.copy if c % 2 == 0 else nc.vector.tensor_copy
+            copy_out(out=bias_sb[:, cols], in_=spread[:])
+
+        for c in range(BLOCKS):
+            cols = slice(c * N_BLOCK, (c + 1) * N_BLOCK)
+            rope_heads = min(BLOCK_HEADS, (QS + KS - c * N_BLOCK) // HD)
+            vector_heads = rope_heads - 1
+            for m in range(TOK_TILES):
+                acc = banks.tile([P, N_BLOCK], F32, tag="bank")
+                for g in range(PASSES):
+                    nc.tensor.matmul_mx(
+                        out=acc[:],
+                        lhsT=x_codes[:, m, g, :].bitcast(FP8X4),
+                        lhsT_scale=x_scales[:, m, g, :],
+                        rhs=w_tiles[(c, g)][:].bitcast(FP8X4),
+                        rhs_scale=w_planes[4 * g : P, cols],
+                        start=(g == 0),
+                        stop=(g == PASSES - 1),
+                    )
+                y = y_pool.tile([P, BLOCK_HEADS, HD], F32)
+                nc.vector.tensor_tensor(
+                    out=y[:].rearrange("p h d -> p (h d)"), in0=acc[:], in1=bias_sb[:, cols], op=ADD
+                )
+                products = products_pool.tile([P, BLOCK_HEADS, RD, 2], F32)
+                shape = [P, vector_heads, RD, 2]
+                nc.vector.tensor_tensor(
+                    out=products[:, 0:vector_heads, :, :],
+                    in0=y[:, 0:vector_heads, 0:RD].unsqueeze(3).to_broadcast(shape),
+                    in1=table_ps[:, m, :, :].unsqueeze(1).to_broadcast(shape),
+                    op=MULT,
+                )
+                shape = [P, 1, RD, 2]
+                nc.gpsimd.tensor_tensor(
+                    out=products[:, vector_heads:rope_heads, :, :],
+                    in0=y[:, vector_heads:rope_heads, 0:RD].unsqueeze(3).to_broadcast(shape),
+                    in1=table_sb[:, m, :, :].unsqueeze(1).to_broadcast(shape),
+                    op=MULT,
+                )
+                pairs = products[:, 0:rope_heads, :, :].rearrange("p h (j s) e -> p h j s e", s=2)
+                nc.gpsimd.tensor_tensor(
+                    out=y[:, 0:rope_heads, 0:RD].rearrange("p h (j e) -> p h j e", e=2),
+                    in0=pairs[:, :, :, 0, :],
+                    in1=pairs[:, :, :, 1, :],
+                    op=ADD,
+                )
+                rows = slice(m * P, (m + 1) * P)
+                if c * N_BLOCK < QS:
+                    heads = slice(c * BLOCK_HEADS, (c + 1) * BLOCK_HEADS)
+                    nc.scalar.dma_start(out=out_0[rows, heads, :], in_=y[:])
+                else:
+                    nc.scalar.dma_start(out=out_1[rows, :, :], in_=y[:, 0:NKV, :])
+                    nc.scalar.dma_start(out=out_2[rows, :, :], in_=y[:, NKV : 2 * NKV, :])

@@ -40,8 +40,8 @@ def tile_selfattention_pa_kernel(
         x_pool = stack.enter_context(tc.tile_pool(name="x", bufs=TOK_TILES))
         grouped_pool = stack.enter_context(tc.tile_pool(name="grouped", bufs=2))
         w_pool = stack.enter_context(tc.tile_pool(name="w", bufs=BLOCKS * PASSES))
-        y_pool = stack.enter_context(tc.tile_pool(name="y", bufs=12))
-        products_pool = stack.enter_context(tc.tile_pool(name="products", bufs=4))
+        y_pool = stack.enter_context(tc.tile_pool(name="y", bufs=5))
+        products_pool = stack.enter_context(tc.tile_pool(name="products", bufs=3))
         banks = stack.enter_context(tc.psum_pool(name="banks", bufs=7))
         table_bank = stack.enter_context(tc.psum_pool(name="table_bank", bufs=1))
 
@@ -140,52 +140,63 @@ def tile_selfattention_pa_kernel(
             copy_out = nc.scalar.copy if c % 2 == 0 else nc.vector.tensor_copy
             copy_out(out=bias_sb[:, cols], in_=spread[:])
 
-        for c in range(BLOCKS):
-            cols = slice(c * N_BLOCK, (c + 1) * N_BLOCK)
-            rope_heads = min(BLOCK_HEADS, (QS + KS - c * N_BLOCK) // HD)
-            vector_heads = rope_heads - 1
+        by_tile = "(m p) h d -> p m h d"
+        blocks = [
+            (c * N_BLOCK, BLOCK_HEADS, True, out_0[:, c * BLOCK_HEADS : (c + 1) * BLOCK_HEADS, :])
+            for c in range(QS // N_BLOCK)
+        ]
+        blocks.append((QS, NKV, True, out_1))
+        blocks.append((QS + KS, NKV, False, out_2))
+
+        for first, heads, rotated, dram in blocks:
+            width = heads * HD
+            cols = slice(first, first + width)
+            w_cols = slice(first % N_BLOCK, first % N_BLOCK + width)
+            vector_heads = heads - 1
+            y = y_pool.tile([P, TOK_TILES, heads, HD], F32, tag="y")
+            if rotated:
+                products = products_pool.tile([P, TOK_TILES, heads, RD, 2], F32, tag="products")
             for m in range(TOK_TILES):
                 acc = banks.tile([P, N_BLOCK], F32, tag="bank")
                 for g in range(PASSES):
                     nc.tensor.matmul_mx(
-                        out=acc[:],
+                        out=acc[:, 0:width],
                         lhsT=x_codes[:, m, g, :].bitcast(FP8X4),
                         lhsT_scale=x_scales[:, m, g, :],
-                        rhs=w_tiles[(c, g)][:].bitcast(FP8X4),
+                        rhs=w_tiles[(first // N_BLOCK, g)][:, w_cols].bitcast(FP8X4),
                         rhs_scale=w_planes[4 * g : P, cols],
                         start=(g == 0),
                         stop=(g == PASSES - 1),
                     )
-                y = y_pool.tile([P, BLOCK_HEADS, HD], F32)
                 nc.vector.tensor_tensor(
-                    out=y[:].rearrange("p h d -> p (h d)"), in0=acc[:], in1=bias_sb[:, cols], op=ADD
+                    out=y[:, m].rearrange("p h d -> p (h d)"),
+                    in0=acc[:, 0:width],
+                    in1=bias_sb[:, cols],
+                    op=ADD,
                 )
-                products = products_pool.tile([P, BLOCK_HEADS, RD, 2], F32)
-                shape = [P, vector_heads, RD, 2]
-                nc.vector.tensor_tensor(
-                    out=products[:, 0:vector_heads, :, :],
-                    in0=y[:, 0:vector_heads, 0:RD].unsqueeze(3).to_broadcast(shape),
-                    in1=table_ps[:, m, :, :].unsqueeze(1).to_broadcast(shape),
+                if rotated:
+                    shape = [P, vector_heads, RD, 2]
+                    nc.vector.tensor_tensor(
+                        out=products[:, m, 0:vector_heads, :, :],
+                        in0=y[:, m, 0:vector_heads, 0:RD].unsqueeze(3).to_broadcast(shape),
+                        in1=table_ps[:, m, :, :].unsqueeze(1).to_broadcast(shape),
+                        op=MULT,
+                    )
+            if rotated:
+                nc.gpsimd.tensor_tensor(
+                    out=products[:, :, vector_heads, :, :],
+                    in0=y[:, :, vector_heads, 0:RD].unsqueeze(3).to_broadcast([P, TOK_TILES, RD, 2]),
+                    in1=table_sb[:],
                     op=MULT,
                 )
-                shape = [P, 1, RD, 2]
+                pairs = products[:].rearrange("p m h (j s) e -> p (m h) j s e", s=2)
+                y_heads = y[:].rearrange("p m h d -> p (m h) d")
                 nc.gpsimd.tensor_tensor(
-                    out=products[:, vector_heads:rope_heads, :, :],
-                    in0=y[:, vector_heads:rope_heads, 0:RD].unsqueeze(3).to_broadcast(shape),
-                    in1=table_sb[:, m, :, :].unsqueeze(1).to_broadcast(shape),
-                    op=MULT,
-                )
-                pairs = products[:, 0:rope_heads, :, :].rearrange("p h (j s) e -> p h j s e", s=2)
-                nc.gpsimd.tensor_tensor(
-                    out=y[:, 0:rope_heads, 0:RD].rearrange("p h (j e) -> p h j e", e=2),
+                    out=y_heads[:, :, 0:RD].rearrange("p a (j e) -> p a j e", e=2),
                     in0=pairs[:, :, :, 0, :],
                     in1=pairs[:, :, :, 1, :],
                     op=ADD,
                 )
-                rows = slice(m * P, (m + 1) * P)
-                if c * N_BLOCK < QS:
-                    heads = slice(c * BLOCK_HEADS, (c + 1) * BLOCK_HEADS)
-                    nc.scalar.dma_start(out=out_0[rows, heads, :], in_=y[:])
-                else:
-                    nc.scalar.dma_start(out=out_1[rows, :, :], in_=y[:, 0:NKV, :])
-                    nc.scalar.dma_start(out=out_2[rows, :, :], in_=y[:, NKV : 2 * NKV, :])
+            dram_tiles = dram.rearrange(by_tile, p=P)
+            for m in range(TOK_TILES):
+                nc.scalar.dma_start(out=dram_tiles[:, m], in_=y[:, m])

@@ -44,6 +44,7 @@ def tile_selfattention_pa_kernel(
         products_pool = stack.enter_context(tc.tile_pool(name="products", bufs=3))
         banks = stack.enter_context(tc.psum_pool(name="banks", bufs=7))
         table_bank = stack.enter_context(tc.psum_pool(name="table_bank", bufs=1))
+        stack.enter_context(tc.manual_schedule())
 
         w_planes = const.tile([P, OUT], U8, align_bytes=64)
         nc.vector.memset(w_planes[:].bitcast(I32), 0)
@@ -71,11 +72,11 @@ def tile_selfattention_pa_kernel(
                 )
                 w_tiles[(c, g)] = w_sb
 
-        nc.scalar.dma_start(out=bias_row[0:1, :], in_=b_qkv.unsqueeze(0))
         cos_sb = const.tile([P, TOK_TILES, RD], BF16)
         sin_sb = const.tile([P, TOK_TILES, RD], BF16)
         nc.scalar.dma_start(out=cos_sb[:], in_=cos.rearrange("(m p) c -> p m c", p=P))
         nc.scalar.dma_start(out=sin_sb[:], in_=sin.rearrange("(m p) c -> p m c", p=P))
+        nc.scalar.dma_start(out=bias_row[0:1, :], in_=b_qkv.unsqueeze(0))
 
         ident_f32 = const.tile([P, P], F32)
         make_identity(nc, ident_f32[:])
@@ -83,6 +84,16 @@ def tile_selfattention_pa_kernel(
         make_identity(nc, ident_bf16[:])
         ones = const.tile([P, P], BF16)
         nc.vector.memset(ones[:], 1.0)
+
+        table_sb = const.tile([P, TOK_TILES, RD, 2], BF16)
+        table_js = table_sb[:].rearrange("p m (j s) e -> p m j s e", s=2)
+        half_rd = RD // 2
+        nc.vector.tensor_copy(out=table_js[:, :, :, 0, 0], in_=cos_sb[:, :, 0:half_rd])
+        nc.vector.tensor_copy(out=table_js[:, :, :, 0, 1], in_=sin_sb[:, :, half_rd:RD])
+        nc.vector.tensor_scalar_mul(
+            out=table_js[:, :, :, 1, 0], in0=sin_sb[:, :, 0:half_rd], scalar1=-1.0
+        )
+        nc.vector.tensor_copy(out=table_js[:, :, :, 1, 1], in_=cos_sb[:, :, half_rd:RD])
 
         x_codes = const.tile([P, TOK_TILES, PASSES, P], U32, align_bytes=64)
         x_scales = const.tile([P, TOK_TILES, PASSES, P], U8, align_bytes=64)
@@ -103,8 +114,7 @@ def tile_selfattention_pa_kernel(
                             x_words[:, WORDS * g + u : WORDS * (g + 1) : 2],
                             ident_f32[:],
                         )
-                copy_out = nc.scalar.copy if half == 0 else nc.vector.tensor_copy
-                copy_out(
+                nc.scalar.copy(
                     out=grouped_words[:, 2 * half : 2 * half + 2, :, :],
                     in_=xt[:].rearrange("p a u r -> p a r u"),
                 )
@@ -114,15 +124,6 @@ def tile_selfattention_pa_kernel(
                 in_=grouped_flat,
             )
 
-        table_sb = const.tile([P, TOK_TILES, RD, 2], BF16)
-        table_js = table_sb[:].rearrange("p m (j s) e -> p m j s e", s=2)
-        half_rd = RD // 2
-        nc.vector.tensor_copy(out=table_js[:, :, :, 0, 0], in_=cos_sb[:, :, 0:half_rd])
-        nc.vector.tensor_copy(out=table_js[:, :, :, 0, 1], in_=sin_sb[:, :, half_rd:RD])
-        nc.vector.tensor_scalar_mul(
-            out=table_js[:, :, :, 1, 0], in0=sin_sb[:, :, 0:half_rd], scalar1=-1.0
-        )
-        nc.vector.tensor_copy(out=table_js[:, :, :, 1, 1], in_=cos_sb[:, :, half_rd:RD])
         table_ps = table_bank.tile([P, TOK_TILES, RD, 2], F32)
         nc.tensor.matmul(
             out=table_ps[:].rearrange("p m i e -> p (m i e)"),
@@ -152,10 +153,21 @@ def tile_selfattention_pa_kernel(
             width = heads * HD
             cols = slice(first, first + width)
             w_cols = slice(first % N_BLOCK, first % N_BLOCK + width)
-            vector_heads = heads - 1
+            gpsimd_heads = heads // BLOCK_HEADS
+            vector_heads = heads - gpsimd_heads
             y = y_pool.tile([P, TOK_TILES, heads, HD], F32, tag="y")
             if rotated:
                 products = products_pool.tile([P, TOK_TILES, heads, RD, 2], F32, tag="products")
+
+            def multiply_on_vector(m):
+                shape = [P, vector_heads, RD, 2]
+                nc.vector.tensor_tensor(
+                    out=products[:, m, 0:vector_heads, :, :],
+                    in0=y[:, m, 0:vector_heads, 0:RD].unsqueeze(3).to_broadcast(shape),
+                    in1=table_ps[:, m, :, :].unsqueeze(1).to_broadcast(shape),
+                    op=MULT,
+                )
+
             for m in range(TOK_TILES):
                 acc = banks.tile([P, N_BLOCK], F32, tag="bank")
                 for g in range(PASSES):
@@ -174,21 +186,20 @@ def tile_selfattention_pa_kernel(
                     in1=bias_sb[:, cols],
                     op=ADD,
                 )
-                if rotated:
-                    shape = [P, vector_heads, RD, 2]
-                    nc.vector.tensor_tensor(
-                        out=products[:, m, 0:vector_heads, :, :],
-                        in0=y[:, m, 0:vector_heads, 0:RD].unsqueeze(3).to_broadcast(shape),
-                        in1=table_ps[:, m, :, :].unsqueeze(1).to_broadcast(shape),
+                if rotated and m > 0:
+                    multiply_on_vector(m - 1)
+            if rotated:
+                multiply_on_vector(TOK_TILES - 1)
+            if rotated:
+                if gpsimd_heads > 0:
+                    nc.gpsimd.tensor_tensor(
+                        out=products[:, :, vector_heads, :, :],
+                        in0=y[:, :, vector_heads, 0:RD]
+                        .unsqueeze(3)
+                        .to_broadcast([P, TOK_TILES, RD, 2]),
+                        in1=table_sb[:],
                         op=MULT,
                     )
-            if rotated:
-                nc.gpsimd.tensor_tensor(
-                    out=products[:, :, vector_heads, :, :],
-                    in0=y[:, :, vector_heads, 0:RD].unsqueeze(3).to_broadcast([P, TOK_TILES, RD, 2]),
-                    in1=table_sb[:],
-                    op=MULT,
-                )
                 pairs = products[:].rearrange("p m h (j s) e -> p (m h) j s e", s=2)
                 y_heads = y[:].rearrange("p m h d -> p (m h) d")
                 nc.gpsimd.tensor_tensor(
@@ -198,5 +209,6 @@ def tile_selfattention_pa_kernel(
                     op=ADD,
                 )
             dram_tiles = dram.rearrange(by_tile, p=P)
+            store_queue = nc.scalar if rotated else nc.sync
             for m in range(TOK_TILES):
-                nc.scalar.dma_start(out=dram_tiles[:, m], in_=y[:, m])
+                store_queue.dma_start(out=dram_tiles[:, m], in_=y[:, m])

@@ -39,7 +39,7 @@ def tile_selfattention_pa_kernel(
         const = stack.enter_context(tc.tile_pool(name="const", bufs=1))
         x_pool = stack.enter_context(tc.tile_pool(name="x", bufs=TOK_TILES))
         grouped_pool = stack.enter_context(tc.tile_pool(name="grouped", bufs=2))
-        w_pool = stack.enter_context(tc.tile_pool(name="w", bufs=BLOCKS * PASSES))
+        w_pool = stack.enter_context(tc.tile_pool(name="w", bufs=BLOCKS))
         y_pool = stack.enter_context(tc.tile_pool(name="y", bufs=5))
         products_pool = stack.enter_context(tc.tile_pool(name="products", bufs=3))
         banks = stack.enter_context(tc.psum_pool(name="banks", bufs=7))
@@ -61,16 +61,19 @@ def tile_selfattention_pa_kernel(
                 out=w_planes[32 * quad : 32 * quad + 16, :].bitcast(I32),
                 in_=W_qkv_scales[:, 4 * quad : 4 * quad + 4, :].bitcast(I32),
             )
-        w_tiles = {}
+        w_tiles = []
+        w_bytes = W_qkv_words.rearrange("g p n t -> p g (n t)")
         for c in range(BLOCKS):
-            for g in range(PASSES):
-                w_sb = w_pool.tile([P, N_BLOCK], U32, align_bytes=64)
-                w_bytes = W_qkv_words[g].rearrange("p n t -> p (n t)")
-                nc.sync.dma_start(
-                    out=w_sb[:].bitcast(I32),
-                    in_=w_bytes[:, 4 * c * N_BLOCK : 4 * (c + 1) * N_BLOCK].bitcast(I32),
-                )
-                w_tiles[(c, g)] = w_sb
+            w_sb = w_pool.tile([P, PASSES, N_BLOCK], U32, align_bytes=64)
+            byte_cols = slice(4 * c * N_BLOCK, 4 * (c + 1) * N_BLOCK)
+            if c == 0:
+                for g in range(PASSES):
+                    nc.sync.dma_start(
+                        out=w_sb[:, g, :].bitcast(I32), in_=w_bytes[:, g, byte_cols].bitcast(I32)
+                    )
+            else:
+                nc.sync.dma_start(out=w_sb[:].bitcast(I32), in_=w_bytes[:, :, byte_cols].bitcast(I32))
+            w_tiles.append(w_sb)
 
         cos_sb = const.tile([P, TOK_TILES, RD], BF16)
         sin_sb = const.tile([P, TOK_TILES, RD], BF16)
@@ -175,7 +178,7 @@ def tile_selfattention_pa_kernel(
                         out=acc[:, 0:width],
                         lhsT=x_codes[:, m, g, :].bitcast(FP8X4),
                         lhsT_scale=x_scales[:, m, g, :],
-                        rhs=w_tiles[(first // N_BLOCK, g)][:, w_cols].bitcast(FP8X4),
+                        rhs=w_tiles[first // N_BLOCK][:, g, w_cols].bitcast(FP8X4),
                         rhs_scale=w_planes[4 * g : P, cols],
                         start=(g == 0),
                         stop=(g == PASSES - 1),
@@ -210,5 +213,8 @@ def tile_selfattention_pa_kernel(
                 )
             dram_tiles = dram.rearrange(by_tile, p=P)
             store_queue = nc.scalar if rotated else nc.sync
-            for m in range(TOK_TILES):
-                store_queue.dma_start(out=dram_tiles[:, m], in_=y[:, m])
+            if heads == BLOCK_HEADS:
+                store_queue.dma_start(out=dram_tiles, in_=y[:])
+            else:
+                for m in range(TOK_TILES):
+                    store_queue.dma_start(out=dram_tiles[:, m], in_=y[:, m])

@@ -25,6 +25,7 @@ N_BLOCK = 512
 BLOCKS = OUT // N_BLOCK
 BLOCK_HEADS = N_BLOCK // HD
 WORDS = K_PASS // 2
+WARM_MATMULS = 4
 
 FLOPS = 2 * T * H * OUT
 
@@ -46,66 +47,89 @@ def tile_selfattention_pa_kernel(
         table_bank = stack.enter_context(tc.psum_pool(name="table_bank", bufs=1))
         stack.enter_context(tc.manual_schedule())
 
+        ident_f32 = const.tile([P, P], F32)
+        make_identity(nc, ident_f32[:])
+        ident_bf16 = const.tile([P, P], BF16)
+        make_identity(nc, ident_bf16[:])
+        zero = const.tile([P, 1], F32)
+        nc.vector.memset(zero[:], 0.0)
+        warm = const.tile([P, N_BLOCK], BF16)
+        nc.vector.memset(warm[:].bitcast(I32), 0)
+        warm_bank = banks.tile([P, N_BLOCK], F32, tag="bank")
+        for repeat in range(WARM_MATMULS):
+            nc.tensor.matmul(out=warm_bank[:], lhsT=warm[:, 0:P], rhs=warm[:], start=True, stop=True)
+        bias_rows = const.tile([P, N_BLOCK], BF16)
+        nc.vector.memset(bias_rows[:].bitcast(I32), 0)
         w_planes = const.tile([P, OUT], U8, align_bytes=64)
         nc.vector.memset(w_planes[:].bitcast(I32), 0)
-        bias_row = const.tile([P, OUT], BF16)
-        nc.vector.memset(bias_row[:].bitcast(I32), 0)
 
         x_tiles = []
         for m in range(TOK_TILES):
             x_sb = x_pool.tile([P, H], BF16)
-            nc.sync.dma_start(out=x_sb[:], in_=hidden_states[m * P : (m + 1) * P, :])
             x_tiles.append(x_sb)
-        for quad in range(4):
-            nc.sync.dma_start(
-                out=w_planes[32 * quad : 32 * quad + 16, :].bitcast(I32),
-                in_=W_qkv_scales[:, 4 * quad : 4 * quad + 4, :].bitcast(I32),
-            )
+
+        def load_x(m, pieces):
+            width = H // pieces
+            for piece in range(pieces):
+                cols = slice(piece * width, (piece + 1) * width)
+                nc.sync.dma_start(out=x_tiles[m][:, cols], in_=hidden_states[m * P : (m + 1) * P, cols])
+
+        def load_scales(cols):
+            for quad in range(4):
+                nc.sync.dma_start(
+                    out=w_planes[32 * quad : 32 * quad + 16, cols].bitcast(I32),
+                    in_=W_qkv_scales[:, 4 * quad : 4 * quad + 4, cols].bitcast(I32),
+                )
+
         w_tiles = []
         w_bytes = W_qkv_words.rearrange("g p n t -> p g (n t)")
         for c in range(BLOCKS):
             w_sb = w_pool.tile([P, PASSES, N_BLOCK], U32, align_bytes=64)
+            w_tiles.append(w_sb)
+
+        def load_w(c, by_pass):
             byte_cols = slice(4 * c * N_BLOCK, 4 * (c + 1) * N_BLOCK)
-            if c == 0:
+            if by_pass:
                 for g in range(PASSES):
                     nc.sync.dma_start(
-                        out=w_sb[:, g, :].bitcast(I32), in_=w_bytes[:, g, byte_cols].bitcast(I32)
+                        out=w_tiles[c][:, g, :].bitcast(I32), in_=w_bytes[:, g, byte_cols].bitcast(I32)
                     )
             else:
-                nc.sync.dma_start(out=w_sb[:].bitcast(I32), in_=w_bytes[:, :, byte_cols].bitcast(I32))
-            w_tiles.append(w_sb)
+                nc.sync.dma_start(out=w_tiles[c][:].bitcast(I32), in_=w_bytes[:, :, byte_cols].bitcast(I32))
+
+        load_x(0, 4)
+        nc.sync.dma_start(out=bias_rows[0:8, :], in_=b_qkv[0 : 8 * N_BLOCK].rearrange("(c n) -> c n", n=N_BLOCK))
+        nc.sync.dma_start(out=bias_rows[8:9, :], in_=b_qkv[8 * N_BLOCK : OUT].unsqueeze(0))
+        load_x(1, 1)
+        load_scales(slice(0, 2 * N_BLOCK))
+        load_w(0, True)
+        load_x(2, 1)
+        load_x(3, 1)
+        load_w(1, False)
+        load_scales(slice(2 * N_BLOCK, OUT))
+        for c in range(2, BLOCKS):
+            load_w(c, False)
 
         cos_sb = const.tile([P, TOK_TILES, RD], BF16)
         sin_sb = const.tile([P, TOK_TILES, RD], BF16)
         nc.scalar.dma_start(out=cos_sb[:], in_=cos.rearrange("(m p) c -> p m c", p=P))
         nc.scalar.dma_start(out=sin_sb[:], in_=sin.rearrange("(m p) c -> p m c", p=P))
-        nc.scalar.dma_start(out=bias_row[0:1, :], in_=b_qkv.unsqueeze(0))
-
-        ident_f32 = const.tile([P, P], F32)
-        make_identity(nc, ident_f32[:])
-        ident_bf16 = const.tile([P, P], BF16)
-        make_identity(nc, ident_bf16[:])
-        ones = const.tile([P, P], BF16)
-        nc.vector.memset(ones[:], 1.0)
-
-        table_sb = const.tile([P, TOK_TILES, RD, 2], BF16)
-        table_js = table_sb[:].rearrange("p m (j s) e -> p m j s e", s=2)
-        half_rd = RD // 2
-        nc.vector.tensor_copy(out=table_js[:, :, :, 0, 0], in_=cos_sb[:, :, 0:half_rd])
-        nc.vector.tensor_copy(out=table_js[:, :, :, 0, 1], in_=sin_sb[:, :, half_rd:RD])
-        nc.vector.tensor_scalar_mul(
-            out=table_js[:, :, :, 1, 0], in0=sin_sb[:, :, 0:half_rd], scalar1=-1.0
-        )
-        nc.vector.tensor_copy(out=table_js[:, :, :, 1, 1], in_=cos_sb[:, :, half_rd:RD])
+        scratch = const.tile([P, 1], F32)
+        nc.scalar.copy(out=scratch[:], in_=zero[:])
 
         x_codes = const.tile([P, TOK_TILES, PASSES, P], U32, align_bytes=64)
         x_scales = const.tile([P, TOK_TILES, PASSES, P], U8, align_bytes=64)
-        for m in range(TOK_TILES):
+        grouped_tiles = {}
+
+        def transpose_x(m):
             x_words = x_tiles[m][:].bitcast(F32)
             grouped = grouped_pool.tile([P, PASSES, P, 4], BF16, align_bytes=64)
-            grouped_flat = grouped[:].rearrange("p g r t -> p (g r t)")
-            grouped_words = grouped_flat.bitcast(F32).rearrange(
-                "p (g r u) -> p g r u", g=PASSES, u=2
+            grouped_tiles[m] = grouped
+            grouped_words = (
+                grouped[:]
+                .rearrange("p g r t -> p (g r t)")
+                .bitcast(F32)
+                .rearrange("p (g r u) -> p g r u", g=PASSES, u=2)
             )
             for half in range(2):
                 xt = banks.tile([P, 2, 2, P], F32, tag="bank")
@@ -121,11 +145,45 @@ def tile_selfattention_pa_kernel(
                     out=grouped_words[:, 2 * half : 2 * half + 2, :, :],
                     in_=xt[:].rearrange("p a u r -> p a r u"),
                 )
+
+        def quantise_x(m):
             nc.vector.quantize_mx(
                 out=x_codes[:, m].rearrange("p g r -> p (g r)").bitcast(FP8X4),
                 scales=x_scales[:, m].rearrange("p g r -> p (g r)"),
-                in_=grouped_flat,
+                in_=grouped_tiles[m][:].rearrange("p g r t -> p (g r t)"),
             )
+
+        bias_sb = const.tile([P, OUT], F32)
+
+        def spread_bias(c):
+            spread = banks.tile([P, N_BLOCK], F32, tag="bank")
+            nc.tensor.matmul(
+                out=spread[:],
+                lhsT=ident_bf16[:, c : c + 1].to_broadcast([P, P]),
+                rhs=bias_rows[:],
+                start=True,
+                stop=True,
+            )
+            copy_out = nc.scalar.copy if c % 2 == 0 else nc.vector.tensor_copy
+            copy_out(out=bias_sb[:, c * N_BLOCK : (c + 1) * N_BLOCK], in_=spread[:])
+
+        transpose_x(0)
+        for c in range(0, 4):
+            spread_bias(c)
+        quantise_x(0)
+        table_sb = const.tile([P, TOK_TILES, RD, 2], BF16)
+        table_js = table_sb[:].rearrange("p m (j s) e -> p m j s e", s=2)
+        half_rd = RD // 2
+        nc.vector.tensor_copy(out=table_js[:, :, :, 0, 0], in_=cos_sb[:, :, 0:half_rd])
+        nc.vector.tensor_copy(out=table_js[:, :, :, 0, 1], in_=sin_sb[:, :, half_rd:RD])
+        nc.vector.tensor_scalar_mul(
+            out=table_js[:, :, :, 1, 0], in0=sin_sb[:, :, 0:half_rd], scalar1=-1.0
+        )
+        nc.vector.tensor_copy(out=table_js[:, :, :, 1, 1], in_=cos_sb[:, :, half_rd:RD])
+        transpose_x(1)
+        for c in range(4, BLOCKS):
+            spread_bias(c)
+        quantise_x(1)
 
         table_ps = table_bank.tile([P, TOK_TILES, RD, 2], F32)
         nc.tensor.matmul(
@@ -136,85 +194,105 @@ def tile_selfattention_pa_kernel(
             stop=True,
         )
 
-        bias_sb = const.tile([P, OUT], F32)
-        for c in range(BLOCKS):
-            cols = slice(c * N_BLOCK, (c + 1) * N_BLOCK)
-            spread = banks.tile([P, N_BLOCK], F32, tag="bank")
-            nc.tensor.matmul(out=spread[:], lhsT=ones[:], rhs=bias_row[:, cols], start=True, stop=True)
-            copy_out = nc.scalar.copy if c % 2 == 0 else nc.vector.tensor_copy
-            copy_out(out=bias_sb[:, cols], in_=spread[:])
-
-        by_tile = "(m p) h d -> p m h d"
+        q_blocks = QS // N_BLOCK
         blocks = [
-            (c * N_BLOCK, BLOCK_HEADS, True, out_0[:, c * BLOCK_HEADS : (c + 1) * BLOCK_HEADS, :])
-            for c in range(QS // N_BLOCK)
+            (
+                c * N_BLOCK,
+                BLOCK_HEADS,
+                True,
+                out_0[:, c * BLOCK_HEADS : (c + 1) * BLOCK_HEADS, :],
+                c == q_blocks - 1,
+                1 if c < q_blocks - 2 else 0,
+            )
+            for c in range(q_blocks)
         ]
-        blocks.append((QS, NKV, True, out_1))
-        blocks.append((QS + KS, NKV, False, out_2))
+        blocks.append((QS, NKV, True, out_1, True, 0))
+        blocks.append((QS + KS, NKV, False, out_2, True, 0))
+        y_tiles = {}
+        products_tiles = {}
 
-        for first, heads, rotated, dram in blocks:
+        def project(b, m):
+            first, heads, rotated, dram, fine, gpsimd_heads = blocks[b]
             width = heads * HD
             cols = slice(first, first + width)
             w_cols = slice(first % N_BLOCK, first % N_BLOCK + width)
-            gpsimd_heads = heads // BLOCK_HEADS
-            vector_heads = heads - gpsimd_heads
-            y = y_pool.tile([P, TOK_TILES, heads, HD], F32, tag="y")
-            if rotated:
-                products = products_pool.tile([P, TOK_TILES, heads, RD, 2], F32, tag="products")
+            if b not in y_tiles:
+                y = y_pool.tile([P, TOK_TILES, heads, HD], F32, tag="y")
+                y_tiles[b] = y
+                if rotated:
+                    products = products_pool.tile([P, TOK_TILES, heads, RD, 2], F32, tag="products")
+                    products_tiles[b] = products
+            acc = banks.tile([P, N_BLOCK], F32, tag="bank")
+            for g in range(PASSES):
+                nc.tensor.matmul_mx(
+                    out=acc[:, 0:width],
+                    lhsT=x_codes[:, m, g, :].bitcast(FP8X4),
+                    lhsT_scale=x_scales[:, m, g, :],
+                    rhs=w_tiles[first // N_BLOCK][:, g, w_cols].bitcast(FP8X4),
+                    rhs_scale=w_planes[4 * g : P, cols],
+                    start=(g == 0),
+                    stop=(g == PASSES - 1),
+                )
+            nc.vector.tensor_tensor(
+                out=y_tiles[b][:, m].rearrange("p h d -> p (h d)"),
+                in0=acc[:, 0:width],
+                in1=bias_sb[:, cols],
+                op=ADD,
+            )
+            if not rotated:
+                nc.sync.dma_start(out=dram.rearrange("(m p) h d -> p m h d", p=P)[:, m], in_=y_tiles[b][:, m])
 
-            def multiply_on_vector(m):
-                shape = [P, vector_heads, RD, 2]
-                nc.vector.tensor_tensor(
-                    out=products[:, m, 0:vector_heads, :, :],
-                    in0=y[:, m, 0:vector_heads, 0:RD].unsqueeze(3).to_broadcast(shape),
-                    in1=table_ps[:, m, :, :].unsqueeze(1).to_broadcast(shape),
+        def finish(b, tiles):
+            first, heads, rotated, dram, fine, gpsimd_heads = blocks[b]
+            y = y_tiles[b]
+            products = products_tiles[b]
+            count = tiles.stop - tiles.start
+            vector_heads = heads - gpsimd_heads
+            if vector_heads < heads:
+                nc.gpsimd.tensor_tensor(
+                    out=products[:, tiles, vector_heads, :, :],
+                    in0=y[:, tiles, vector_heads, 0:RD].unsqueeze(3).to_broadcast([P, count, RD, 2]),
+                    in1=table_sb[:, tiles],
                     op=MULT,
                 )
+            pairs = products[:, tiles].rearrange("p m h (j s) e -> p (m h) j s e", s=2)
+            y_heads = y[:, tiles].rearrange("p m h d -> p (m h) d")
+            nc.gpsimd.tensor_tensor(
+                out=y_heads[:, :, 0:RD].rearrange("p a (j e) -> p a j e", e=2),
+                in0=pairs[:, :, :, 0, :],
+                in1=pairs[:, :, :, 1, :],
+                op=ADD,
+            )
+            nc.scalar.dma_start(out=dram.rearrange("(m p) h d -> p m h d", p=P)[:, tiles], in_=y[:, tiles])
 
-            for m in range(TOK_TILES):
-                acc = banks.tile([P, N_BLOCK], F32, tag="bank")
-                for g in range(PASSES):
-                    nc.tensor.matmul_mx(
-                        out=acc[:, 0:width],
-                        lhsT=x_codes[:, m, g, :].bitcast(FP8X4),
-                        lhsT_scale=x_scales[:, m, g, :],
-                        rhs=w_tiles[first // N_BLOCK][:, g, w_cols].bitcast(FP8X4),
-                        rhs_scale=w_planes[4 * g : P, cols],
-                        start=(g == 0),
-                        stop=(g == PASSES - 1),
-                    )
-                nc.vector.tensor_tensor(
-                    out=y[:, m].rearrange("p h d -> p (h d)"),
-                    in0=acc[:, 0:width],
-                    in1=bias_sb[:, cols],
-                    op=ADD,
-                )
-                if rotated and m > 0:
-                    multiply_on_vector(m - 1)
-            if rotated:
-                multiply_on_vector(TOK_TILES - 1)
-            if rotated:
-                if gpsimd_heads > 0:
-                    nc.gpsimd.tensor_tensor(
-                        out=products[:, :, vector_heads, :, :],
-                        in0=y[:, :, vector_heads, 0:RD]
-                        .unsqueeze(3)
-                        .to_broadcast([P, TOK_TILES, RD, 2]),
-                        in1=table_sb[:],
-                        op=MULT,
-                    )
-                pairs = products[:].rearrange("p m h (j s) e -> p (m h) j s e", s=2)
-                y_heads = y[:].rearrange("p m h d -> p (m h) d")
-                nc.gpsimd.tensor_tensor(
-                    out=y_heads[:, :, 0:RD].rearrange("p a (j e) -> p a j e", e=2),
-                    in0=pairs[:, :, :, 0, :],
-                    in1=pairs[:, :, :, 1, :],
-                    op=ADD,
-                )
-            dram_tiles = dram.rearrange(by_tile, p=P)
-            store_queue = nc.scalar if rotated else nc.sync
-            if heads == BLOCK_HEADS:
-                store_queue.dma_start(out=dram_tiles, in_=y[:])
-            else:
-                for m in range(TOK_TILES):
-                    store_queue.dma_start(out=dram_tiles[:, m], in_=y[:, m])
+        def rotate(b, m):
+            first, heads, rotated, dram, fine, gpsimd_heads = blocks[b]
+            if not rotated:
+                return
+            vector_heads = heads - gpsimd_heads
+            shape = [P, vector_heads, RD, 2]
+            nc.vector.tensor_tensor(
+                out=products_tiles[b][:, m, 0:vector_heads, :, :],
+                in0=y_tiles[b][:, m, 0:vector_heads, 0:RD].unsqueeze(3).to_broadcast(shape),
+                in1=table_ps[:, m, :, :].unsqueeze(1).to_broadcast(shape),
+                op=MULT,
+            )
+            if fine:
+                finish(b, slice(m, m + 1))
+            elif m == TOK_TILES - 1:
+                finish(b, slice(0, TOK_TILES))
+
+        jobs = [(0, 0), (0, 1), (1, 0), (1, 1), (0, 2), (0, 3), (1, 2), (1, 3)]
+        jobs.extend([(b, m) for b in range(2, len(blocks)) for m in range(TOK_TILES)])
+        behind = None
+        for step, (b, m) in enumerate(jobs):
+            project(b, m)
+            if behind is not None:
+                rotate(behind[0], behind[1])
+            behind = (b, m)
+            if step == 1:
+                transpose_x(2)
+                transpose_x(3)
+                quantise_x(2)
+                quantise_x(3)
+        rotate(behind[0], behind[1])

@@ -40,9 +40,9 @@ def tile_selfattention_pa_kernel(
         const = stack.enter_context(tc.tile_pool(name="const", bufs=1))
         x_pool = stack.enter_context(tc.tile_pool(name="x", bufs=TOK_TILES))
         grouped_pool = stack.enter_context(tc.tile_pool(name="grouped", bufs=2))
-        w_pool = stack.enter_context(tc.tile_pool(name="w", bufs=BLOCKS))
-        y_pool = stack.enter_context(tc.tile_pool(name="y", bufs=5))
-        products_pool = stack.enter_context(tc.tile_pool(name="products", bufs=3))
+        w_pool = stack.enter_context(tc.tile_pool(name="w", bufs=1))
+        y_pool = stack.enter_context(tc.tile_pool(name="y", bufs=8))
+        products_pool = stack.enter_context(tc.tile_pool(name="products", bufs=4))
         banks = stack.enter_context(tc.psum_pool(name="banks", bufs=7))
         table_bank = stack.enter_context(tc.psum_pool(name="table_bank", bufs=1))
         stack.enter_context(tc.manual_schedule())
@@ -81,34 +81,33 @@ def tile_selfattention_pa_kernel(
                     in_=W_qkv_scales[:, 4 * quad : 4 * quad + 4, cols].bitcast(I32),
                 )
 
-        w_tiles = []
         w_bytes = W_qkv_words.rearrange("g p n t -> p g (n t)")
-        for c in range(BLOCKS):
-            w_sb = w_pool.tile([P, PASSES, N_BLOCK], U32, align_bytes=64)
-            w_tiles.append(w_sb)
+        w_place = {}
 
-        def load_w(c, by_pass):
-            byte_cols = slice(4 * c * N_BLOCK, 4 * (c + 1) * N_BLOCK)
+        def load_w(c, blocks_wide, by_pass):
+            w_sb = w_pool.tile([P, PASSES, blocks_wide * N_BLOCK], U32, align_bytes=64, name="w%d" % c)
+            for i in range(blocks_wide):
+                w_place[c + i] = (w_sb, i * N_BLOCK)
+            byte_cols = slice(4 * c * N_BLOCK, 4 * (c + blocks_wide) * N_BLOCK)
             if by_pass:
                 for g in range(PASSES):
-                    nc.sync.dma_start(
-                        out=w_tiles[c][:, g, :].bitcast(I32), in_=w_bytes[:, g, byte_cols].bitcast(I32)
-                    )
+                    nc.sync.dma_start(out=w_sb[:, g, :].bitcast(I32), in_=w_bytes[:, g, byte_cols].bitcast(I32))
             else:
-                nc.sync.dma_start(out=w_tiles[c][:].bitcast(I32), in_=w_bytes[:, :, byte_cols].bitcast(I32))
+                nc.sync.dma_start(out=w_sb[:].bitcast(I32), in_=w_bytes[:, :, byte_cols].bitcast(I32))
 
         load_x(0, 4)
         nc.sync.dma_start(out=bias_rows[0:8, :], in_=b_qkv[0 : 8 * N_BLOCK].rearrange("(c n) -> c n", n=N_BLOCK))
         nc.sync.dma_start(out=bias_rows[8:9, :], in_=b_qkv[8 * N_BLOCK : OUT].unsqueeze(0))
         load_x(1, 1)
         load_scales(slice(0, 2 * N_BLOCK))
-        load_w(0, True)
+        load_w(0, 1, True)
         load_x(2, 1)
         load_x(3, 1)
-        load_w(1, False)
+        load_w(1, 1, False)
         load_scales(slice(2 * N_BLOCK, OUT))
-        for c in range(2, BLOCKS):
-            load_w(c, False)
+        load_w(2, 1, False)
+        for c in range(3, BLOCKS, 2):
+            load_w(c, 2, False)
 
         cos_sb = const.tile([P, TOK_TILES, RD], BF16)
         sin_sb = const.tile([P, TOK_TILES, RD], BF16)
@@ -215,7 +214,8 @@ def tile_selfattention_pa_kernel(
             first, heads, rotated, dram, fine, gpsimd_heads = blocks[b]
             width = heads * HD
             cols = slice(first, first + width)
-            w_cols = slice(first % N_BLOCK, first % N_BLOCK + width)
+            w_sb, w_first = w_place[first // N_BLOCK]
+            w_cols = slice(w_first + first % N_BLOCK, w_first + first % N_BLOCK + width)
             if b not in y_tiles:
                 y = y_pool.tile([P, TOK_TILES, heads, HD], F32, tag="y")
                 y_tiles[b] = y
@@ -228,7 +228,7 @@ def tile_selfattention_pa_kernel(
                     out=acc[:, 0:width],
                     lhsT=x_codes[:, m, g, :].bitcast(FP8X4),
                     lhsT_scale=x_scales[:, m, g, :],
-                    rhs=w_tiles[first // N_BLOCK][:, g, w_cols].bitcast(FP8X4),
+                    rhs=w_sb[:, g, w_cols].bitcast(FP8X4),
                     rhs_scale=w_planes[4 * g : P, cols],
                     start=(g == 0),
                     stop=(g == PASSES - 1),

@@ -263,7 +263,8 @@ def tile_selfattention_pa_kernel(
                 in1=pairs[:, :, :, 1, :],
                 op=ADD,
             )
-            nc.scalar.dma_start(out=dram.rearrange("(m p) h d -> p m h d", p=P)[:, tiles], in_=y[:, tiles])
+            store_queue = nc.scalar if fine else nc.sync
+            store_queue.dma_start(out=dram.rearrange("(m p) h d -> p m h d", p=P)[:, tiles], in_=y[:, tiles])
 
         def rotate(b, m):
             first, heads, rotated, dram, fine, gpsimd_heads = blocks[b]

@@ -60,6 +60,8 @@ def tile_selfattention_pa_kernel(
             nc.tensor.matmul(out=warm_bank[:], lhsT=warm[:, 0:P], rhs=warm[:], start=True, stop=True)
         bias_rows = const.tile([P, N_BLOCK], BF16)
         nc.vector.memset(bias_rows[:].bitcast(I32), 0)
+        bias_last = const.tile([P, N_BLOCK], BF16)
+        nc.vector.memset(bias_last[:].bitcast(I32), 0)
         w_planes = const.tile([P, OUT], U8, align_bytes=64)
         nc.vector.memset(w_planes[:].bitcast(I32), 0)
 
@@ -95,15 +97,15 @@ def tile_selfattention_pa_kernel(
             else:
                 nc.sync.dma_start(out=w_sb[:].bitcast(I32), in_=w_bytes[:, :, byte_cols].bitcast(I32))
 
-        load_x(0, 4)
+        load_x(0, 2)
         nc.sync.dma_start(out=bias_rows[0:8, :], in_=b_qkv[0 : 8 * N_BLOCK].rearrange("(c n) -> c n", n=N_BLOCK))
-        nc.sync.dma_start(out=bias_rows[8:9, :], in_=b_qkv[8 * N_BLOCK : OUT].unsqueeze(0))
         load_x(1, 1)
-        load_scales(slice(0, 2 * N_BLOCK))
-        load_w(0, 1, True)
         load_x(2, 1)
         load_x(3, 1)
+        load_scales(slice(0, 2 * N_BLOCK))
+        load_w(0, 1, True)
         load_w(1, 1, False)
+        nc.sync.dma_start(out=bias_last[0:1, :], in_=b_qkv[8 * N_BLOCK : OUT].unsqueeze(0))
         load_scales(slice(2 * N_BLOCK, OUT))
         load_w(2, 1, False)
         for c in range(3, BLOCKS, 2):
@@ -158,8 +160,8 @@ def tile_selfattention_pa_kernel(
             spread = banks.tile([P, N_BLOCK], F32, tag="bank")
             nc.tensor.matmul(
                 out=spread[:],
-                lhsT=ident_bf16[:, c : c + 1].to_broadcast([P, P]),
-                rhs=bias_rows[:],
+                lhsT=ident_bf16[:, c % 8 : c % 8 + 1].to_broadcast([P, P]),
+                rhs=bias_rows[:] if c < 8 else bias_last[:],
                 start=True,
                 stop=True,
             )
@@ -180,9 +182,15 @@ def tile_selfattention_pa_kernel(
         )
         nc.vector.tensor_copy(out=table_js[:, :, :, 1, 1], in_=cos_sb[:, :, half_rd:RD])
         transpose_x(1)
-        for c in range(4, BLOCKS):
-            spread_bias(c)
+        spread_bias(4)
+        spread_bias(5)
         quantise_x(1)
+        transpose_x(2)
+        spread_bias(6)
+        quantise_x(2)
+        transpose_x(3)
+        spread_bias(7)
+        quantise_x(3)
 
         table_ps = table_bank.tile([P, TOK_TILES, RD, 2], F32)
         nc.tensor.matmul(
@@ -283,7 +291,7 @@ def tile_selfattention_pa_kernel(
             elif m == TOK_TILES - 1:
                 finish(b, slice(0, TOK_TILES))
 
-        jobs = [(0, 0), (0, 1), (1, 0), (1, 1), (0, 2), (0, 3), (1, 2), (1, 3)]
+        jobs = [(0, 0), (0, 1), (0, 2), (0, 3), (1, 0), (1, 1), (1, 2), (1, 3)]
         jobs.extend([(b, m) for b in range(2, len(blocks)) for m in range(TOK_TILES)])
         behind = None
         for step, (b, m) in enumerate(jobs):
@@ -291,9 +299,6 @@ def tile_selfattention_pa_kernel(
             if behind is not None:
                 rotate(behind[0], behind[1])
             behind = (b, m)
-            if step == 1:
-                transpose_x(2)
-                transpose_x(3)
-                quantise_x(2)
-                quantise_x(3)
+            if step == 2:
+                spread_bias(BLOCKS - 1)
         rotate(behind[0], behind[1])

@@ -26,6 +26,8 @@ BLOCKS = OUT // N_BLOCK
 BLOCK_HEADS = N_BLOCK // HD
 WORDS = K_PASS // 2
 WARM_MATMULS = 4
+LAST_BIAS_STEP = 8
+TABLE_STEP = 5
 
 FLOPS = 2 * T * H * OUT
 
@@ -97,7 +99,7 @@ def tile_selfattention_pa_kernel(
             else:
                 nc.sync.dma_start(out=w_sb[:].bitcast(I32), in_=w_bytes[:, :, byte_cols].bitcast(I32))
 
-        load_x(0, 2)
+        load_x(0, 4)
         nc.sync.dma_start(out=bias_rows[0:8, :], in_=b_qkv[0 : 8 * N_BLOCK].rearrange("(c n) -> c n", n=N_BLOCK))
         load_x(1, 1)
         load_x(2, 1)
@@ -105,16 +107,18 @@ def tile_selfattention_pa_kernel(
         load_scales(slice(0, 2 * N_BLOCK))
         load_w(0, 1, True)
         load_w(1, 1, False)
-        nc.sync.dma_start(out=bias_last[0:1, :], in_=b_qkv[8 * N_BLOCK : OUT].unsqueeze(0))
-        load_scales(slice(2 * N_BLOCK, OUT))
-        load_w(2, 1, False)
-        for c in range(3, BLOCKS, 2):
-            load_w(c, 2, False)
-
         cos_sb = const.tile([P, TOK_TILES, RD], BF16)
         sin_sb = const.tile([P, TOK_TILES, RD], BF16)
-        nc.scalar.dma_start(out=cos_sb[:], in_=cos.rearrange("(m p) c -> p m c", p=P))
-        nc.scalar.dma_start(out=sin_sb[:], in_=sin.rearrange("(m p) c -> p m c", p=P))
+        nc.sync.dma_start(out=cos_sb[:], in_=cos.rearrange("(m p) c -> p m c", p=P))
+        nc.sync.dma_start(out=sin_sb[:], in_=sin.rearrange("(m p) c -> p m c", p=P))
+        nc.sync.dma_start(out=bias_last[0:1, :], in_=b_qkv[8 * N_BLOCK : OUT].unsqueeze(0))
+        load_scales(slice(2 * N_BLOCK, 4 * N_BLOCK))
+        load_w(2, 1, False)
+        load_w(3, 2, False)
+        load_scales(slice(4 * N_BLOCK, OUT))
+        for c in range(5, BLOCKS, 2):
+            load_w(c, 2, False)
+
         scratch = const.tile([P, 1], F32)
         nc.scalar.copy(out=scratch[:], in_=zero[:])
 
@@ -172,15 +176,6 @@ def tile_selfattention_pa_kernel(
         for c in range(0, 4):
             spread_bias(c)
         quantise_x(0)
-        table_sb = const.tile([P, TOK_TILES, RD, 2], BF16)
-        table_js = table_sb[:].rearrange("p m (j s) e -> p m j s e", s=2)
-        half_rd = RD // 2
-        nc.vector.tensor_copy(out=table_js[:, :, :, 0, 0], in_=cos_sb[:, :, 0:half_rd])
-        nc.vector.tensor_copy(out=table_js[:, :, :, 0, 1], in_=sin_sb[:, :, half_rd:RD])
-        nc.vector.tensor_scalar_mul(
-            out=table_js[:, :, :, 1, 0], in0=sin_sb[:, :, 0:half_rd], scalar1=-1.0
-        )
-        nc.vector.tensor_copy(out=table_js[:, :, :, 1, 1], in_=cos_sb[:, :, half_rd:RD])
         transpose_x(1)
         spread_bias(4)
         spread_bias(5)
@@ -192,14 +187,25 @@ def tile_selfattention_pa_kernel(
         spread_bias(7)
         quantise_x(3)
 
+        table_sb = const.tile([P, TOK_TILES, RD, 2], BF16)
         table_ps = table_bank.tile([P, TOK_TILES, RD, 2], F32)
-        nc.tensor.matmul(
-            out=table_ps[:].rearrange("p m i e -> p (m i e)"),
-            lhsT=ident_bf16[:],
-            rhs=table_sb[:].rearrange("p m i e -> p (m i e)"),
-            start=True,
-            stop=True,
-        )
+
+        def build_table():
+            table_js = table_sb[:].rearrange("p m (j s) e -> p m j s e", s=2)
+            half_rd = RD // 2
+            nc.vector.tensor_copy(out=table_js[:, :, :, 0, 0], in_=cos_sb[:, :, 0:half_rd])
+            nc.vector.tensor_copy(out=table_js[:, :, :, 0, 1], in_=sin_sb[:, :, half_rd:RD])
+            nc.vector.tensor_scalar_mul(out=table_js[:, :, :, 1, 0], in0=sin_sb[:, :, 0:half_rd], scalar1=-1.0)
+            nc.vector.tensor_copy(out=table_js[:, :, :, 1, 1], in_=cos_sb[:, :, half_rd:RD])
+
+        def copy_table():
+            nc.tensor.matmul(
+                out=table_ps[:].rearrange("p m i e -> p (m i e)"),
+                lhsT=ident_bf16[:],
+                rhs=table_sb[:].rearrange("p m i e -> p (m i e)"),
+                start=True,
+                stop=True,
+            )
 
         q_blocks = QS // N_BLOCK
         blocks = [
@@ -293,12 +299,17 @@ def tile_selfattention_pa_kernel(
 
         jobs = [(0, 0), (0, 1), (0, 2), (0, 3), (1, 0), (1, 1), (1, 2), (1, 3)]
         jobs.extend([(b, m) for b in range(2, len(blocks)) for m in range(TOK_TILES)])
-        behind = None
+        behind = []
         for step, (b, m) in enumerate(jobs):
             project(b, m)
-            if behind is not None:
-                rotate(behind[0], behind[1])
-            behind = (b, m)
-            if step == 2:
+            behind.append((b, m))
+            if step == LAST_BIAS_STEP:
                 spread_bias(BLOCKS - 1)
-        rotate(behind[0], behind[1])
+            if step == TABLE_STEP - 2:
+                build_table()
+            if step == TABLE_STEP:
+                copy_table()
+            while step >= TABLE_STEP and len(behind) > 1:
+                rotate(behind[0][0], behind[0][1])
+                behind.remove(behind[0])
+        rotate(behind[0][0], behind[0][1])

from contextlib import ExitStack

import concourse.mybir as mybir
from concourse.masks import make_identity

F32 = mybir.dt.float32
BF16 = mybir.dt.bfloat16
I32 = mybir.dt.int32
U32 = mybir.dt.uint32
U8 = mybir.dt.uint8
FP8X4 = mybir.dt.float8_e4m3fn_x4
ADD = mybir.AluOpType.add
MULT = mybir.AluOpType.mult

P = 128
T, H = 512, 2048
NQ, NKV, HD = 32, 2, 128
RD = HD // 2
QS, KS = NQ * HD, NKV * HD
OUT = QS + 2 * KS
K_PASS = 4 * P
PASSES = H // K_PASS
TOK_TILES = T // P
N_BLOCK = 512
BLOCKS = OUT // N_BLOCK
BLOCK_HEADS = N_BLOCK // HD
WORDS = K_PASS // 2
WARM_MATMULS = 4
LAST_BIAS_STEP = 8
TABLE_STEP = 5

FLOPS = 2 * T * H * OUT

assert QS % N_BLOCK == 0 and 2 * KS == N_BLOCK


def tile_selfattention_pa_kernel(
    tc, hidden_states, cos, sin, W_qkv_words, W_qkv_scales, b_qkv, out_0, out_1, out_2
):
    nc = tc.nc
    with ExitStack() as stack:
        const = stack.enter_context(tc.tile_pool(name="const", bufs=1))
        x_pool = stack.enter_context(tc.tile_pool(name="x", bufs=TOK_TILES))
        grouped_pool = stack.enter_context(tc.tile_pool(name="grouped", bufs=2))
        w_pool = stack.enter_context(tc.tile_pool(name="w", bufs=1))
        y_pool = stack.enter_context(tc.tile_pool(name="y", bufs=8))
        products_pool = stack.enter_context(tc.tile_pool(name="products", bufs=4))
        banks = stack.enter_context(tc.psum_pool(name="banks", bufs=7))
        table_bank = stack.enter_context(tc.psum_pool(name="table_bank", bufs=1))
        stack.enter_context(tc.manual_schedule())

        ident_f32 = const.tile([P, P], F32)
        make_identity(nc, ident_f32[:])
        ident_bf16 = const.tile([P, P], BF16)
        make_identity(nc, ident_bf16[:])
        zero = const.tile([P, 1], F32)
        nc.vector.memset(zero[:], 0.0)
        warm = const.tile([P, N_BLOCK], BF16)
        nc.vector.memset(warm[:].bitcast(I32), 0)
        warm_bank = banks.tile([P, N_BLOCK], F32, tag="bank")
        for repeat in range(WARM_MATMULS):
            nc.tensor.matmul(out=warm_bank[:], lhsT=warm[:, 0:P], rhs=warm[:], start=True, stop=True)
        bias_rows = const.tile([P, N_BLOCK], BF16)
        nc.vector.memset(bias_rows[:].bitcast(I32), 0)
        bias_last = const.tile([P, N_BLOCK], BF16)
        nc.vector.memset(bias_last[:].bitcast(I32), 0)
        w_planes = const.tile([P, OUT], U8, align_bytes=64)
        nc.vector.memset(w_planes[:].bitcast(I32), 0)

        x_tiles = []
        for m in range(TOK_TILES):
            x_sb = x_pool.tile([P, H], BF16)
            x_tiles.append(x_sb)

        def load_x(m, pieces):
            width = H // pieces
            for piece in range(pieces):
                cols = slice(piece * width, (piece + 1) * width)
                nc.sync.dma_start(out=x_tiles[m][:, cols], in_=hidden_states[m * P : (m + 1) * P, cols])

        def load_scales(cols):
            for quad in range(4):
                nc.sync.dma_start(
                    out=w_planes[32 * quad : 32 * quad + 16, cols].bitcast(I32),
                    in_=W_qkv_scales[:, 4 * quad : 4 * quad + 4, cols].bitcast(I32),
                )

        w_bytes = W_qkv_words.rearrange("g p n t -> p g (n t)")
        w_place = {}

        def load_w(c, blocks_wide, by_pass):
            w_sb = w_pool.tile([P, PASSES, blocks_wide * N_BLOCK], U32, align_bytes=64, name="w%d" % c)
            for i in range(blocks_wide):
                w_place[c + i] = (w_sb, i * N_BLOCK)
            byte_cols = slice(4 * c * N_BLOCK, 4 * (c + blocks_wide) * N_BLOCK)
            if by_pass:
                for g in range(PASSES):
                    nc.sync.dma_start(out=w_sb[:, g, :].bitcast(I32), in_=w_bytes[:, g, byte_cols].bitcast(I32))
            else:
                nc.sync.dma_start(out=w_sb[:].bitcast(I32), in_=w_bytes[:, :, byte_cols].bitcast(I32))

        load_x(0, 4)
        nc.sync.dma_start(out=bias_rows[0:8, :], in_=b_qkv[0 : 8 * N_BLOCK].rearrange("(c n) -> c n", n=N_BLOCK))
        load_x(1, 1)
        load_x(2, 1)
        load_x(3, 1)
        load_scales(slice(0, 2 * N_BLOCK))
        load_w(0, 1, True)
        load_w(1, 1, False)
        cos_sb = const.tile([P, TOK_TILES, RD], BF16)
        sin_sb = const.tile([P, TOK_TILES, RD], BF16)
        nc.sync.dma_start(out=cos_sb[:], in_=cos.rearrange("(m p) c -> p m c", p=P))
        nc.sync.dma_start(out=sin_sb[:], in_=sin.rearrange("(m p) c -> p m c", p=P))
        nc.sync.dma_start(out=bias_last[0:1, :], in_=b_qkv[8 * N_BLOCK : OUT].unsqueeze(0))
        load_scales(slice(2 * N_BLOCK, 4 * N_BLOCK))
        load_w(2, 1, False)
        load_w(3, 2, False)
        load_scales(slice(4 * N_BLOCK, OUT))
        for c in range(5, BLOCKS, 2):
            load_w(c, 2, False)

        scratch = const.tile([P, 1], F32)
        nc.scalar.copy(out=scratch[:], in_=zero[:])

        x_codes = const.tile([P, TOK_TILES, PASSES, P], U32, align_bytes=64)
        x_scales = const.tile([P, TOK_TILES, PASSES, P], U8, align_bytes=64)
        grouped_tiles = {}

        def transpose_x(m):
            x_words = x_tiles[m][:].bitcast(F32)
            grouped = grouped_pool.tile([P, PASSES, P, 4], BF16, align_bytes=64)
            grouped_tiles[m] = grouped
            grouped_words = (
                grouped[:]
                .rearrange("p g r t -> p (g r t)")
                .bitcast(F32)
                .rearrange("p (g r u) -> p g r u", g=PASSES, u=2)
            )
            for half in range(2):
                xt = banks.tile([P, 2, 2, P], F32, tag="bank")
                for a in range(2):
                    g = 2 * half + a
                    for u in range(2):
                        nc.tensor.transpose(
                            xt[:, a, u, :],
                            x_words[:, WORDS * g + u : WORDS * (g + 1) : 2],
                            ident_f32[:],
                        )
                nc.scalar.copy(
                    out=grouped_words[:, 2 * half : 2 * half + 2, :, :],
                    in_=xt[:].rearrange("p a u r -> p a r u"),
                )

        def quantise_x(m):
            nc.vector.quantize_mx(
                out=x_codes[:, m].rearrange("p g r -> p (g r)").bitcast(FP8X4),
                scales=x_scales[:, m].rearrange("p g r -> p (g r)"),
                in_=grouped_tiles[m][:].rearrange("p g r t -> p (g r t)"),
            )

        bias_sb = const.tile([P, OUT], F32)

        def spread_bias(c):
            spread = banks.tile([P, N_BLOCK], F32, tag="bank")
            nc.tensor.matmul(
                out=spread[:],
                lhsT=ident_bf16[:, c % 8 : c % 8 + 1].to_broadcast([P, P]),
                rhs=bias_rows[:] if c < 8 else bias_last[:],
                start=True,
                stop=True,
            )
            copy_out = nc.scalar.copy if c % 2 == 0 else nc.vector.tensor_copy
            copy_out(out=bias_sb[:, c * N_BLOCK : (c + 1) * N_BLOCK], in_=spread[:])

        transpose_x(0)
        for c in range(0, 4):
            spread_bias(c)
        quantise_x(0)
        transpose_x(1)
        spread_bias(4)
        spread_bias(5)
        quantise_x(1)
        transpose_x(2)
        spread_bias(6)
        quantise_x(2)
        transpose_x(3)
        spread_bias(7)
        quantise_x(3)

        table_sb = const.tile([P, TOK_TILES, RD, 2], BF16)
        table_ps = table_bank.tile([P, TOK_TILES, RD, 2], F32)

        def build_table():
            table_js = table_sb[:].rearrange("p m (j s) e -> p m j s e", s=2)
            half_rd = RD // 2
            nc.vector.tensor_copy(out=table_js[:, :, :, 0, 0], in_=cos_sb[:, :, 0:half_rd])
            nc.vector.tensor_copy(out=table_js[:, :, :, 0, 1], in_=sin_sb[:, :, half_rd:RD])
            nc.vector.tensor_scalar_mul(out=table_js[:, :, :, 1, 0], in0=sin_sb[:, :, 0:half_rd], scalar1=-1.0)
            nc.vector.tensor_copy(out=table_js[:, :, :, 1, 1], in_=cos_sb[:, :, half_rd:RD])

        def copy_table():
            nc.tensor.matmul(
                out=table_ps[:].rearrange("p m i e -> p (m i e)"),
                lhsT=ident_bf16[:],
                rhs=table_sb[:].rearrange("p m i e -> p (m i e)"),
                start=True,
                stop=True,
            )

        q_blocks = QS // N_BLOCK
        blocks = [
            (
                c * N_BLOCK,
                BLOCK_HEADS,
                True,
                out_0[:, c * BLOCK_HEADS : (c + 1) * BLOCK_HEADS, :],
                c == q_blocks - 1,
                1 if c < q_blocks - 2 else 0,
            )
            for c in range(q_blocks)
        ]
        blocks.append((QS, NKV, True, out_1, True, 0))
        blocks.append((QS + KS, NKV, False, out_2, True, 0))
        y_tiles = {}
        products_tiles = {}

        def project(b, m):
            first, heads, rotated, dram, fine, gpsimd_heads = blocks[b]
            width = heads * HD
            cols = slice(first, first + width)
            w_sb, w_first = w_place[first // N_BLOCK]
            w_cols = slice(w_first + first % N_BLOCK, w_first + first % N_BLOCK + width)
            if b not in y_tiles:
                y = y_pool.tile([P, TOK_TILES, heads, HD], F32, tag="y")
                y_tiles[b] = y
                if rotated:
                    products = products_pool.tile([P, TOK_TILES, heads, RD, 2], F32, tag="products")
                    products_tiles[b] = products
            acc = banks.tile([P, N_BLOCK], F32, tag="bank")
            for g in range(PASSES):
                nc.tensor.matmul_mx(
                    out=acc[:, 0:width],
                    lhsT=x_codes[:, m, g, :].bitcast(FP8X4),
                    lhsT_scale=x_scales[:, m, g, :],
                    rhs=w_sb[:, g, w_cols].bitcast(FP8X4),
                    rhs_scale=w_planes[4 * g : P, cols],
                    start=(g == 0),
                    stop=(g == PASSES - 1),
                )
            nc.vector.tensor_tensor(
                out=y_tiles[b][:, m].rearrange("p h d -> p (h d)"),
                in0=acc[:, 0:width],
                in1=bias_sb[:, cols],
                op=ADD,
            )
            if not rotated:
                nc.sync.dma_start(out=dram.rearrange("(m p) h d -> p m h d", p=P)[:, m], in_=y_tiles[b][:, m])

        def finish(b, tiles):
            first, heads, rotated, dram, fine, gpsimd_heads = blocks[b]
            y = y_tiles[b]
            products = products_tiles[b]
            count = tiles.stop - tiles.start
            vector_heads = heads - gpsimd_heads
            if vector_heads < heads:
                nc.gpsimd.tensor_tensor(
                    out=products[:, tiles, vector_heads, :, :],
                    in0=y[:, tiles, vector_heads, 0:RD].unsqueeze(3).to_broadcast([P, count, RD, 2]),
                    in1=table_sb[:, tiles],
                    op=MULT,
                )
            pairs = products[:, tiles].rearrange("p m h (j s) e -> p (m h) j s e", s=2)
            y_heads = y[:, tiles].rearrange("p m h d -> p (m h) d")
            nc.gpsimd.tensor_tensor(
                out=y_heads[:, :, 0:RD].rearrange("p a (j e) -> p a j e", e=2),
                in0=pairs[:, :, :, 0, :],
                in1=pairs[:, :, :, 1, :],
                op=ADD,
            )
            store_queue = nc.scalar if fine else nc.sync
            store_queue.dma_start(out=dram.rearrange("(m p) h d -> p m h d", p=P)[:, tiles], in_=y[:, tiles])

        def rotate(b, m):
            first, heads, rotated, dram, fine, gpsimd_heads = blocks[b]
            if not rotated:
                return
            vector_heads = heads - gpsimd_heads
            shape = [P, vector_heads, RD, 2]
            nc.vector.tensor_tensor(
                out=products_tiles[b][:, m, 0:vector_heads, :, :],
                in0=y_tiles[b][:, m, 0:vector_heads, 0:RD].unsqueeze(3).to_broadcast(shape),
                in1=table_ps[:, m, :, :].unsqueeze(1).to_broadcast(shape),
                op=MULT,
            )
            if fine:
                finish(b, slice(m, m + 1))
            elif m == TOK_TILES - 1:
                finish(b, slice(0, TOK_TILES))

        jobs = [(0, 0), (0, 1), (0, 2), (0, 3), (1, 0), (1, 1), (1, 2), (1, 3)]
        jobs.extend([(b, m) for b in range(2, len(blocks)) for m in range(TOK_TILES)])
        behind = []
        for step, (b, m) in enumerate(jobs):
            project(b, m)
            behind.append((b, m))
            if step == LAST_BIAS_STEP:
                spread_bias(BLOCKS - 1)
            if step == TABLE_STEP - 2:
                build_table()
            if step == TABLE_STEP:
                copy_table()
            while step >= TABLE_STEP and len(behind) > 1:
                rotate(behind[0][0], behind[0][1])
                behind.remove(behind[0])
        rotate(behind[0][0], behind[0][1])
